import numpy as np
import ml_dtypes


def mxq(x, axis, fmt="e4m3"):
    dtype, down = {"e4m3": (ml_dtypes.float8_e4m3fn, 7), "e5m2": (ml_dtypes.float8_e5m2, 14)}[fmt]
    v = np.moveaxis(np.asarray(x, np.float32).astype(ml_dtypes.bfloat16).astype(np.float64), axis, -1)
    blocks = v.reshape(v.shape[:-1] + (-1, 32))
    amax = np.abs(blocks).max(-1, keepdims=True)
    byte = np.maximum(np.where(amax > 0, np.frexp(amax)[1] - 1 + 127, 0) - down, 1)
    scale = np.exp2(byte - 127.0)
    codes = (blocks / scale).astype(np.float32).astype(dtype).astype(np.float64)
    return np.moveaxis((codes * scale).reshape(v.shape), -1, axis)


WIDE = False


def mx_kscale(k):
    if not WIDE:
        return np.ones(k)
    levels = np.array([10, -10, 5, -5, 0])
    a = np.random.permutation(np.resize(levels, k // 512 * 4)).reshape(k // 512, 4)
    idx = np.arange(k)
    return np.exp2(a[idx // 512, idx % 128 // 32])


BF16 = ml_dtypes.bfloat16


def bf(x):
    return np.asarray(x, np.float32).astype(BF16)


def f64(x):
    return np.asarray(x).astype(np.float64)


B, IN, HID, PROJ, H, KC = 8192, 128, 512, 512, 4, 4
BH = HID // H
EPS = 1e-5


def silu(v):
    return v / (1.0 + np.exp(-v))


def groupnorm(v, w, b):
    r = v.reshape(B, H, BH)
    mu = r.mean(-1, keepdims=True)
    var = ((r - mu) ** 2).mean(-1, keepdims=True)
    rn = (r - mu) / np.sqrt(var + EPS)
    return rn.reshape(B, HID) * w + b


def setup_inputs():
    s, t = mx_kscale(PROJ), mx_kscale(HID)
    r = np.random.standard_normal
    return {"h_t": bf(r((B, HID)) * 0.5 / np.sqrt(HID)), "x_conv": bf(silu(r((B, PROJ))) * s),
            "x_right": bf(r((B, HID))), "x": bf(r((B, IN))),
            "gn_w": bf((1.0 + 0.1 * r(HID)) * t), "gn_b": bf(0.2 * r(HID) * t),
            "skip_w": bf(r((PROJ, HID)) * 1.5 / np.sqrt(PROJ) / s[:, None] * t[None, :]), "skip_b": bf(0.2 * r(HID) * t),
            "down_w": bf(r((HID, IN)) / np.sqrt(HID) / t[:, None]), "down_b": bf(0.2 * r(IN))}


def reference(h_t, x_conv, x_right, x, gn_w, gn_b, skip_w, skip_b, down_w, down_b):
    x_skip = (mxq(f64(x_conv), 1, "e4m3") @ mxq(f64(skip_w), 0, "e4m3")) + f64(skip_b)
    g = (groupnorm(f64(h_t), f64(gn_w), f64(gn_b)) + x_skip) * silu(f64(x_right))
    y = (mxq(g, 1, "e4m3") @ mxq(f64(down_w), 0, "e4m3")) + f64(down_b)
    return y + f64(x)

@@ -1,0 +1,253 @@
+from contextlib import ExitStack
+
+import concourse.mybir as mybir
+from concourse.masks import make_identity
+
+F32 = mybir.dt.float32
+BF16 = mybir.dt.bfloat16
+U32 = mybir.dt.uint32
+U8 = mybir.dt.uint8
+FP8X4 = mybir.dt.float8_e4m3fn_x4
+ALU = mybir.AluOpType
+ACT = mybir.ActivationFunctionType
+
+P = 128
+PACK = 4
+B, IN, HID, PROJ = 8192, 128, 512, 512
+GROUPS = 4
+GROUP = HID // GROUPS
+EPS = 1e-5
+TILES = 4
+BLOCK = TILES * P
+N_BLOCKS = B // BLOCK
+HALF = TILES // 2
+
+FLOPS = 2 * B * PROJ * HID + 2 * B * HID * IN
+
+
+def quantise(nc, codes, scales, grouped):
+    nc.vector.quantize_mx(out=codes.bitcast(FP8X4), scales=scales, in_=grouped)
+
+
+def tile_mlstmblock_pc_t_kernel(
+    tc, h_t, x_conv, x_right, x, gn_w, gn_b, skip_w, skip_b, down_w, down_b, out
+):
+    nc = tc.nc
+    h_blocks = h_t.rearrange("(b p t) c -> b p t c", p=P, t=TILES)
+    xc_blocks = x_conv.rearrange("(b p t) c -> b p t c", p=P, t=TILES)
+    xr_blocks = x_right.rearrange("(b p t) c -> b p t c", p=P, t=TILES)
+    x_blocks = x.rearrange("(b p t) c -> b p t c", p=P, t=TILES)
+    out_blocks = out.rearrange("(b p t) c -> b p t c", p=P, t=TILES)
+
+    with ExitStack() as ctx:
+        consts = ctx.enter_context(tc.tile_pool(name="consts", bufs=1))
+        loads = ctx.enter_context(tc.tile_pool(name="loads", bufs=3))
+        work = ctx.enter_context(tc.tile_pool(name="work", bufs=2))
+        small = ctx.enter_context(tc.tile_pool(name="small", bufs=3))
+        psum_xc = ctx.enter_context(tc.psum_pool(name="psum_xc", bufs=1))
+        psum_xr = ctx.enter_context(tc.psum_pool(name="psum_xr", bufs=2))
+        psum_n = ctx.enter_context(tc.psum_pool(name="psum_n", bufs=2))
+        psum_skip = ctx.enter_context(tc.psum_pool(name="psum_skip", bufs=2))
+        psum_y = ctx.enter_context(tc.psum_pool(name="psum_y", bufs=1))
+
+        ident_bf16 = consts.tile([P, P], BF16)
+        make_identity(nc, ident_bf16[:])
+        ident_f32 = consts.tile([P, P], F32)
+        make_identity(nc, ident_f32[:])
+
+        skip_raw = consts.tile([P, PACK, HID], BF16)
+        for u in range(2):
+            nc.sync.dma_start(
+                out=skip_raw[:, 2 * u : 2 * u + 2, :],
+                in_=skip_w[256 * u : 256 * u + 256, :].rearrange("(p e) c -> p e c", e=2),
+            )
+        skip_grouped = consts.tile([P, HID, PACK], BF16, align_bytes=64)
+        nc.vector.tensor_copy(out=skip_grouped[:], in_=skip_raw[:].rearrange("p k c -> p c k"))
+        skip_codes = consts.tile([P, HID], U32, align_bytes=64)
+        skip_scales = consts.tile([P, HID], U8, align_bytes=64)
+
+        down_raw = consts.tile([P, PACK, IN], BF16)
+        nc.sync.dma_start(out=down_raw[:], in_=down_w.rearrange("(j p) c -> p j c", p=P))
+        down_grouped = consts.tile([P, IN, PACK], BF16, align_bytes=64)
+        nc.vector.tensor_copy(out=down_grouped[:], in_=down_raw[:].rearrange("p k c -> p c k"))
+        down_codes = consts.tile([P, IN], U32, align_bytes=64)
+        down_scales = consts.tile([P, IN], U8, align_bytes=64)
+        quantise(nc, skip_codes[:], skip_scales[:], skip_grouped[:].rearrange("p c k -> p (c k)"))
+        quantise(nc, down_codes[:], down_scales[:], down_grouped[:].rearrange("p c k -> p (c k)"))
+
+        vec_rows = consts.tile([P, P], BF16)
+        nc.vector.memset(vec_rows[:], 0.0)
+        for i, vec in enumerate((gn_w, gn_b, skip_b)):
+            nc.sync.dma_start(
+                out=vec_rows[GROUPS * i : GROUPS * (i + 1), :], in_=vec.rearrange("(j p) -> j p", p=P)
+            )
+        vec_t = psum_xr.tile([P, HALF, GROUPS, P], BF16, tag="xr_t")
+        nc.tensor.transpose(vec_t[:, 0, 0, :], vec_rows[:], ident_bf16[:])
+        vec_cols = consts.tile([P, 3 * GROUPS], F32)
+        nc.vector.tensor_copy(out=vec_cols[:], in_=vec_t[:, 0, 0, 0 : 3 * GROUPS])
+        gain = vec_cols[:, 0:GROUPS]
+        shift = consts.tile([P, GROUPS], F32)
+        nc.vector.tensor_tensor(
+            out=shift[:], in0=vec_cols[:, GROUPS : 2 * GROUPS], in1=vec_cols[:, 2 * GROUPS : 3 * GROUPS], op=ALU.add
+        )
+
+        down_b_all = consts.tile([P, IN], BF16)
+        nc.gpsimd.dma_start(out=down_b_all[:], in_=down_b.partition_broadcast(P))
+        neg_half = consts.tile([P, TILES * GROUPS, 1], F32)
+        nc.vector.memset(neg_half[:], -0.5)
+
+        for b in range(N_BLOCKS):
+            h_blk = loads.tile([P, TILES, HID], BF16)
+            nc.sync.dma_start(out=h_blk[:], in_=h_blocks[b])
+            xc_blk = loads.tile([P, TILES, PROJ], BF16)
+            nc.sync.dma_start(out=xc_blk[:], in_=xc_blocks[b])
+            xr_blk = loads.tile([P, TILES, HID], BF16)
+            nc.sync.dma_start(out=xr_blk[:], in_=xr_blocks[b])
+            x_blk = loads.tile([P, TILES, IN], BF16)
+            nc.sync.dma_start(out=x_blk[:], in_=x_blocks[b])
+
+            stats = small.tile([P, TILES * GROUPS, 6], F32)
+            for t in range(TILES):
+                for j in range(GROUPS):
+                    nc.vector.bn_stats(
+                        out=stats[:, t * GROUPS + j, :], in_=h_blk[:, t, j * GROUP : (j + 1) * GROUP]
+                    )
+            mean_even, m2_even = stats[:, :, 1:2], stats[:, :, 2:3]
+            mean_odd, m2_odd = stats[:, :, 4:5], stats[:, :, 5:6]
+            mean_sum = small.tile([P, TILES * GROUPS, 1], F32)
+            nc.vector.tensor_tensor(out=mean_sum[:], in0=mean_even, in1=mean_odd, op=ALU.add)
+            mean_diff = small.tile([P, TILES * GROUPS, 1], F32)
+            nc.vector.tensor_tensor(out=mean_diff[:], in0=mean_even, in1=mean_odd, op=ALU.subtract)
+            m2_eps = small.tile([P, TILES * GROUPS, 1], F32)
+            nc.vector.scalar_tensor_tensor(
+                out=m2_eps[:], in0=m2_even, scalar=GROUP * EPS, in1=m2_odd, op0=ALU.add, op1=ALU.add
+            )
+            between = small.tile([P, TILES * GROUPS, 1], F32)
+            nc.vector.scalar_tensor_tensor(
+                out=between[:], in0=mean_diff[:], scalar=0.25, in1=mean_diff[:], op0=ALU.mult, op1=ALU.mult
+            )
+            var_eps = small.tile([P, TILES * GROUPS, 1], F32)
+            nc.vector.scalar_tensor_tensor(
+                out=var_eps[:], in0=m2_eps[:], scalar=1.0 / GROUP, in1=between[:], op0=ALU.mult, op1=ALU.add
+            )
+            rstd = small.tile([P, TILES * GROUPS, 1], F32)
+            nc.gpsimd.tensor_tensor(out=rstd[:], in0=var_eps[:], in1=neg_half[:], op=ALU.pow)
+            neg_mean = small.tile([P, TILES * GROUPS, 1], F32)
+            nc.gpsimd.tensor_scalar(
+                out=neg_mean[:], in0=mean_sum[:], scalar1=-0.5, scalar2=0.0, op0=ALU.mult, op1=ALU.add
+            )
+            neg_mean_rstd = small.tile([P, TILES * GROUPS, 1], F32)
+            nc.gpsimd.tensor_tensor(out=neg_mean_rstd[:], in0=neg_mean[:], in1=rstd[:], op=ALU.mult)
+
+            norm = work.tile([P, TILES, HID], F32)
+            for t in range(TILES):
+                for j in range(GROUPS):
+                    cols = slice(j * GROUP, (j + 1) * GROUP)
+                    nc.scalar.activation(
+                        out=norm[:, t, cols],
+                        in_=h_blk[:, t, cols],
+                        func=ACT.Identity,
+                        scale=rstd[:, t * GROUPS + j, :],
+                        bias=neg_mean_rstd[:, t * GROUPS + j, :],
+                    )
+
+            xc_words = xc_blk[:].bitcast(F32)
+            xc_grouped = work.tile([P, TILES, P, PACK], BF16, align_bytes=64)
+            xc_grouped_words = xc_grouped[:].bitcast(F32)
+            for half in range(TILES // HALF):
+                xc_t = psum_xc.tile([P, HALF, 2, P], F32)
+                for i in range(HALF):
+                    for u in range(2):
+                        nc.tensor.transpose(
+                            xc_t[:, i, u, :], xc_words[:, half * HALF + i, u * P : (u + 1) * P], ident_f32[:]
+                        )
+                nc.scalar.copy(
+                    out=xc_grouped_words[:, half * HALF : (half + 1) * HALF, :, :],
+                    in_=xc_t[:].rearrange("p i u r -> p i r u"),
+                )
+            xc_codes = work.tile([P, TILES * P], U32, align_bytes=64)
+            xc_scales = work.tile([P, TILES * P], U8, align_bytes=64)
+            quantise(nc, xc_codes[:], xc_scales[:], xc_grouped[:].rearrange("p t r k -> p (t r k)"))
+
+            gate = work.tile([P, TILES, P, GROUPS], F32)
+            for half in range(TILES // HALF):
+                xr_t = psum_xr.tile([P, HALF, GROUPS, P], BF16)
+                for i in range(HALF):
+                    for j in range(GROUPS):
+                        nc.tensor.transpose(
+                            xr_t[:, i, j, :], xr_blk[:, half * HALF + i, j * P : (j + 1) * P], ident_bf16[:]
+                        )
+                nc.scalar.activation(
+                    out=gate[:, half * HALF : (half + 1) * HALF, :, :],
+                    in_=xr_t[:].rearrange("p i j r -> p i r j"),
+                    func=ACT.Silu,
+                )
+
+            gn = work.tile([P, GROUPS, TILES, P], F32)
+            for j in range(GROUPS):
+                norm_t = psum_n.tile([P, TILES, P], F32)
+                for t in range(TILES):
+                    nc.tensor.transpose(norm_t[:, t, :], norm[:, t, j * P : (j + 1) * P], ident_f32[:])
+                nc.scalar.activation(
+                    out=gn[:, j, :, :],
+                    in_=norm_t[:],
+                    func=ACT.Identity,
+                    scale=gain[:, j : j + 1],
+                    bias=shift[:, j : j + 1],
+                )
+
+            summed = work.tile([P, TILES, P, GROUPS], F32)
+            for t in range(TILES):
+                rows = slice(t * P, (t + 1) * P)
+                skip_t = psum_skip.tile([P, GROUPS, P], F32)
+                for j in range(GROUPS):
+                    cols = slice(j * P, (j + 1) * P)
+                    nc.tensor.matmul_mx(
+                        out=skip_t[:, j, :],
+                        lhsT=skip_codes[:, cols].bitcast(FP8X4),
+                        lhsT_scale=skip_scales[:, cols],
+                        rhs=xc_codes[:, rows].bitcast(FP8X4),
+                        rhs_scale=xc_scales[:, rows],
+                        start=True,
+                        stop=True,
+                    )
+                nc.vector.tensor_tensor(
+                    out=summed[:, t, :, :],
+                    in0=skip_t[:].rearrange("p j r -> p r j"),
+                    in1=gn[:, :, t, :].rearrange("p j r -> p r j"),
+                    op=ALU.add,
+                )
+
+            g_grouped = work.tile([P, TILES * P * GROUPS], BF16, align_bytes=64)
+            nc.vector.tensor_tensor(
+                out=g_grouped[:],
+                in0=summed[:].rearrange("p t r j -> p (t r j)"),
+                in1=gate[:].rearrange("p t r j -> p (t r j)"),
+                op=ALU.mult,
+            )
+            g_codes = work.tile([P, TILES * P], U32, align_bytes=64)
+            g_scales = work.tile([P, TILES * P], U8, align_bytes=64)
+            quantise(nc, g_codes[:], g_scales[:], g_grouped[:])
+
+            y = psum_y.tile([P, TILES, IN], F32)
+            for t in range(TILES):
+                rows = slice(t * P, (t + 1) * P)
+                nc.tensor.matmul_mx(
+                    out=y[:, t, :],
+                    lhsT=g_codes[:, rows].bitcast(FP8X4),
+                    lhsT_scale=g_scales[:, rows],
+                    rhs=down_codes[:].bitcast(FP8X4),
+                    rhs_scale=down_scales[:],
+                    start=True,
+                    stop=True,
+                )
+            residual = work.tile([P, TILES, IN], F32)
+            nc.gpsimd.tensor_tensor(
+                out=residual[:],
+                in0=x_blk[:],
+                in1=down_b_all[:].unsqueeze(1).to_broadcast([P, TILES, IN]),
+                op=ALU.add,
+            )
+            result = work.tile([P, TILES, IN], F32)
+            nc.vector.tensor_tensor(out=result[:], in0=y[:], in1=residual[:], op=ALU.add)
+            nc.sync.dma_start(out=out_blocks[b], in_=result[:])

@@ -43,12 +43,12 @@ def tile_mlstmblock_pc_t_kernel(
         consts = ctx.enter_context(tc.tile_pool(name="consts", bufs=1))
         loads = ctx.enter_context(tc.tile_pool(name="loads", bufs=3))
         work = ctx.enter_context(tc.tile_pool(name="work", bufs=2))
-        small = ctx.enter_context(tc.tile_pool(name="small", bufs=3))
-        psum_xc = ctx.enter_context(tc.psum_pool(name="psum_xc", bufs=1))
+        held = ctx.enter_context(tc.tile_pool(name="held", bufs=3))
+        small = ctx.enter_context(tc.tile_pool(name="small", bufs=4))
         psum_xr = ctx.enter_context(tc.psum_pool(name="psum_xr", bufs=2))
         psum_n = ctx.enter_context(tc.psum_pool(name="psum_n", bufs=2))
         psum_skip = ctx.enter_context(tc.psum_pool(name="psum_skip", bufs=2))
-        psum_y = ctx.enter_context(tc.psum_pool(name="psum_y", bufs=1))
+        psum_misc = ctx.enter_context(tc.psum_pool(name="psum_misc", bufs=2))
 
         ident_bf16 = consts.tile([P, P], BF16)
         make_identity(nc, ident_bf16[:])
@@ -57,7 +57,7 @@ def tile_mlstmblock_pc_t_kernel(
 
         skip_raw = consts.tile([P, PACK, HID], BF16)
         for u in range(2):
-            nc.sync.dma_start(
+            nc.scalar.dma_start(
                 out=skip_raw[:, 2 * u : 2 * u + 2, :],
                 in_=skip_w[256 * u : 256 * u + 256, :].rearrange("(p e) c -> p e c", e=2),
             )
@@ -67,7 +67,7 @@ def tile_mlstmblock_pc_t_kernel(
         skip_scales = consts.tile([P, HID], U8, align_bytes=64)
 
         down_raw = consts.tile([P, PACK, IN], BF16)
-        nc.sync.dma_start(out=down_raw[:], in_=down_w.rearrange("(j p) c -> p j c", p=P))
+        nc.scalar.dma_start(out=down_raw[:], in_=down_w.rearrange("(j p) c -> p j c", p=P))
         down_grouped = consts.tile([P, IN, PACK], BF16, align_bytes=64)
         nc.vector.tensor_copy(out=down_grouped[:], in_=down_raw[:].rearrange("p k c -> p c k"))
         down_codes = consts.tile([P, IN], U32, align_bytes=64)
@@ -78,7 +78,7 @@ def tile_mlstmblock_pc_t_kernel(
         vec_rows = consts.tile([P, P], BF16)
         nc.vector.memset(vec_rows[:], 0.0)
         for i, vec in enumerate((gn_w, gn_b, skip_b)):
-            nc.sync.dma_start(
+            nc.gpsimd.dma_start(
                 out=vec_rows[GROUPS * i : GROUPS * (i + 1), :], in_=vec.rearrange("(j p) -> j p", p=P)
             )
         vec_t = psum_xr.tile([P, HALF, GROUPS, P], BF16, tag="xr_t")
@@ -96,22 +96,34 @@ def tile_mlstmblock_pc_t_kernel(
         neg_half = consts.tile([P, TILES * GROUPS, 1], F32)
         nc.vector.memset(neg_half[:], -0.5)
 
-        for b in range(N_BLOCKS):
-            h_blk = loads.tile([P, TILES, HID], BF16)
+        tiles = {}
+
+        def load_h_and_x(b):
+            h_blk = loads.tile([P, TILES, HID], BF16, bufs=4)
             nc.sync.dma_start(out=h_blk[:], in_=h_blocks[b])
+            x_blk = loads.tile([P, TILES, IN], BF16)
+            nc.sync.dma_start(out=x_blk[:], in_=x_blocks[b])
+            tiles["h", b], tiles["x", b] = h_blk, x_blk
+
+        def load_x_conv_and_x_right(b):
             xc_blk = loads.tile([P, TILES, PROJ], BF16)
             nc.sync.dma_start(out=xc_blk[:], in_=xc_blocks[b])
             xr_blk = loads.tile([P, TILES, HID], BF16)
             nc.sync.dma_start(out=xr_blk[:], in_=xr_blocks[b])
-            x_blk = loads.tile([P, TILES, IN], BF16)
-            nc.sync.dma_start(out=x_blk[:], in_=x_blocks[b])
+            tiles["xc", b], tiles["xr", b] = xc_blk, xr_blk
 
-            stats = small.tile([P, TILES * GROUPS, 6], F32)
-            for t in range(TILES):
-                for j in range(GROUPS):
-                    nc.vector.bn_stats(
-                        out=stats[:, t * GROUPS + j, :], in_=h_blk[:, t, j * GROUP : (j + 1) * GROUP]
-                    )
+        def group_stats(b, t):
+            if t == 0:
+                stats = small.tile([P, TILES * GROUPS, 6], F32)
+                tiles["stats", b] = stats
+            for j in range(GROUPS):
+                nc.vector.bn_stats(
+                    out=tiles["stats", b][:, t * GROUPS + j, :],
+                    in_=tiles["h", b][:, t, j * GROUP : (j + 1) * GROUP],
+                )
+
+        def join_halves_sums(b):
+            stats = tiles["stats", b]
             mean_even, m2_even = stats[:, :, 1:2], stats[:, :, 2:3]
             mean_odd, m2_odd = stats[:, :, 4:5], stats[:, :, 5:6]
             mean_sum = small.tile([P, TILES * GROUPS, 1], F32)
@@ -122,132 +134,227 @@ def tile_mlstmblock_pc_t_kernel(
             nc.vector.scalar_tensor_tensor(
                 out=m2_eps[:], in0=m2_even, scalar=GROUP * EPS, in1=m2_odd, op0=ALU.add, op1=ALU.add
             )
+            tiles["mean_sum", b], tiles["mean_diff", b], tiles["m2_eps", b] = mean_sum, mean_diff, m2_eps
+
+        def join_halves_between(b):
             between = small.tile([P, TILES * GROUPS, 1], F32)
             nc.vector.scalar_tensor_tensor(
-                out=between[:], in0=mean_diff[:], scalar=0.25, in1=mean_diff[:], op0=ALU.mult, op1=ALU.mult
+                out=between[:],
+                in0=tiles["mean_diff", b][:],
+                scalar=0.25,
+                in1=tiles["mean_diff", b][:],
+                op0=ALU.mult,
+                op1=ALU.mult,
             )
+            tiles["between", b] = between
+
+        def join_halves_variance(b):
             var_eps = small.tile([P, TILES * GROUPS, 1], F32)
             nc.vector.scalar_tensor_tensor(
-                out=var_eps[:], in0=m2_eps[:], scalar=1.0 / GROUP, in1=between[:], op0=ALU.mult, op1=ALU.add
+                out=var_eps[:],
+                in0=tiles["m2_eps", b][:],
+                scalar=1.0 / GROUP,
+                in1=tiles["between", b][:],
+                op0=ALU.mult,
+                op1=ALU.add,
             )
+            tiles["var_eps", b] = var_eps
+
+        def rstd_and_residual(b):
             rstd = small.tile([P, TILES * GROUPS, 1], F32)
-            nc.gpsimd.tensor_tensor(out=rstd[:], in0=var_eps[:], in1=neg_half[:], op=ALU.pow)
+            nc.gpsimd.tensor_tensor(out=rstd[:], in0=tiles["var_eps", b][:], in1=neg_half[:], op=ALU.pow)
             neg_mean = small.tile([P, TILES * GROUPS, 1], F32)
             nc.gpsimd.tensor_scalar(
-                out=neg_mean[:], in0=mean_sum[:], scalar1=-0.5, scalar2=0.0, op0=ALU.mult, op1=ALU.add
+                out=neg_mean[:], in0=tiles["mean_sum", b][:], scalar1=-0.5, scalar2=0.0, op0=ALU.mult, op1=ALU.add
             )
             neg_mean_rstd = small.tile([P, TILES * GROUPS, 1], F32)
             nc.gpsimd.tensor_tensor(out=neg_mean_rstd[:], in0=neg_mean[:], in1=rstd[:], op=ALU.mult)
+            tiles["rstd", b], tiles["neg_mean_rstd", b] = rstd, neg_mean_rstd
+            residual = held.tile([P, TILES, IN], F32, bufs=6)
+            nc.gpsimd.tensor_tensor(
+                out=residual[:],
+                in0=tiles["x", b][:],
+                in1=down_b_all[:].unsqueeze(1).to_broadcast([P, TILES, IN]),
+                op=ALU.add,
+            )
+            tiles["residual", b] = residual
 
-            norm = work.tile([P, TILES, HID], F32)
-            for t in range(TILES):
-                for j in range(GROUPS):
-                    cols = slice(j * GROUP, (j + 1) * GROUP)
-                    nc.scalar.activation(
-                        out=norm[:, t, cols],
-                        in_=h_blk[:, t, cols],
-                        func=ACT.Identity,
-                        scale=rstd[:, t * GROUPS + j, :],
-                        bias=neg_mean_rstd[:, t * GROUPS + j, :],
-                    )
-
-            xc_words = xc_blk[:].bitcast(F32)
-            xc_grouped = work.tile([P, TILES, P, PACK], BF16, align_bytes=64)
-            xc_grouped_words = xc_grouped[:].bitcast(F32)
-            for half in range(TILES // HALF):
-                xc_t = psum_xc.tile([P, HALF, 2, P], F32)
-                for i in range(HALF):
-                    for u in range(2):
-                        nc.tensor.transpose(
-                            xc_t[:, i, u, :], xc_words[:, half * HALF + i, u * P : (u + 1) * P], ident_f32[:]
-                        )
-                nc.scalar.copy(
-                    out=xc_grouped_words[:, half * HALF : (half + 1) * HALF, :, :],
-                    in_=xc_t[:].rearrange("p i u r -> p i r u"),
-                )
-            xc_codes = work.tile([P, TILES * P], U32, align_bytes=64)
-            xc_scales = work.tile([P, TILES * P], U8, align_bytes=64)
-            quantise(nc, xc_codes[:], xc_scales[:], xc_grouped[:].rearrange("p t r k -> p (t r k)"))
-
-            gate = work.tile([P, TILES, P, GROUPS], F32)
-            for half in range(TILES // HALF):
-                xr_t = psum_xr.tile([P, HALF, GROUPS, P], BF16)
-                for i in range(HALF):
-                    for j in range(GROUPS):
-                        nc.tensor.transpose(
-                            xr_t[:, i, j, :], xr_blk[:, half * HALF + i, j * P : (j + 1) * P], ident_bf16[:]
-                        )
-                nc.scalar.activation(
-                    out=gate[:, half * HALF : (half + 1) * HALF, :, :],
-                    in_=xr_t[:].rearrange("p i j r -> p i r j"),
-                    func=ACT.Silu,
-                )
-
-            gn = work.tile([P, GROUPS, TILES, P], F32)
+        def normalise(b, t):
+            if t == 0:
+                norm = work.tile([P, TILES, HID], F32)
+                tiles["norm", b] = norm
             for j in range(GROUPS):
-                norm_t = psum_n.tile([P, TILES, P], F32)
-                for t in range(TILES):
-                    nc.tensor.transpose(norm_t[:, t, :], norm[:, t, j * P : (j + 1) * P], ident_f32[:])
+                cols = slice(j * GROUP, (j + 1) * GROUP)
                 nc.scalar.activation(
-                    out=gn[:, j, :, :],
-                    in_=norm_t[:],
+                    out=tiles["norm", b][:, t, cols],
+                    in_=tiles["h", b][:, t, cols],
                     func=ACT.Identity,
-                    scale=gain[:, j : j + 1],
-                    bias=shift[:, j : j + 1],
+                    scale=tiles["rstd", b][:, t * GROUPS + j, :],
+                    bias=tiles["neg_mean_rstd", b][:, t * GROUPS + j, :],
                 )
 
-            summed = work.tile([P, TILES, P, GROUPS], F32)
-            for t in range(TILES):
-                rows = slice(t * P, (t + 1) * P)
-                skip_t = psum_skip.tile([P, GROUPS, P], F32)
-                for j in range(GROUPS):
-                    cols = slice(j * P, (j + 1) * P)
-                    nc.tensor.matmul_mx(
-                        out=skip_t[:, j, :],
-                        lhsT=skip_codes[:, cols].bitcast(FP8X4),
-                        lhsT_scale=skip_scales[:, cols],
-                        rhs=xc_codes[:, rows].bitcast(FP8X4),
-                        rhs_scale=xc_scales[:, rows],
-                        start=True,
-                        stop=True,
+        def transpose_x_conv(b, half):
+            xc_words = tiles["xc", b][:].bitcast(F32)
+            xc_t = psum_misc.tile([P, HALF, 2, P], F32, tag="misc")
+            for i in range(HALF):
+                for u in range(2):
+                    nc.tensor.transpose(
+                        xc_t[:, i, u, :], xc_words[:, half * HALF + i, u * P : (u + 1) * P], ident_f32[:]
                     )
-                nc.vector.tensor_tensor(
-                    out=summed[:, t, :, :],
-                    in0=skip_t[:].rearrange("p j r -> p r j"),
-                    in1=gn[:, :, t, :].rearrange("p j r -> p r j"),
-                    op=ALU.add,
-                )
+            tiles["xc_t", b, half] = xc_t
 
-            g_grouped = work.tile([P, TILES * P * GROUPS], BF16, align_bytes=64)
+        def group_x_conv(b, half):
+            if half == 0:
+                xc_grouped = work.tile([P, TILES, P, PACK], BF16, align_bytes=64)
+                tiles["xc_grouped", b] = xc_grouped
+            nc.scalar.copy(
+                out=tiles["xc_grouped", b][:].bitcast(F32)[:, half * HALF : (half + 1) * HALF, :, :],
+                in_=tiles["xc_t", b, half][:].rearrange("p i u r -> p i r u"),
+            )
+
+        def quantise_x_conv(b):
+            xc_codes = held.tile([P, TILES * P], U32, align_bytes=64)
+            xc_scales = held.tile([P, TILES * P], U8, align_bytes=64)
+            quantise(nc, xc_codes[:], xc_scales[:], tiles["xc_grouped", b][:].rearrange("p t r k -> p (t r k)"))
+            tiles["xc_codes", b], tiles["xc_scales", b] = xc_codes, xc_scales
+
+        def transpose_x_right(b, half):
+            xr_t = psum_xr.tile([P, HALF, GROUPS, P], BF16)
+            for i in range(HALF):
+                for j in range(GROUPS):
+                    nc.tensor.transpose(
+                        xr_t[:, i, j, :], tiles["xr", b][:, half * HALF + i, j * P : (j + 1) * P], ident_bf16[:]
+                    )
+            tiles["xr_t", b, half] = xr_t
+
+        def silu_gate(b, half):
+            if half == 0:
+                gate = held.tile([P, TILES, P, GROUPS], F32)
+                tiles["gate", b] = gate
+            nc.scalar.activation(
+                out=tiles["gate", b][:, half * HALF : (half + 1) * HALF, :, :],
+                in_=tiles["xr_t", b, half][:].rearrange("p i j r -> p i r j"),
+                func=ACT.Silu,
+            )
+
+        def transpose_norm(b, j):
+            norm_t = psum_n.tile([P, TILES, P], F32)
+            for t in range(TILES):
+                nc.tensor.transpose(norm_t[:, t, :], tiles["norm", b][:, t, j * P : (j + 1) * P], ident_f32[:])
+            tiles["norm_t", b, j] = norm_t
+
+        def gain_and_biases(b, j):
+            if j == 0:
+                gn = work.tile([P, GROUPS, TILES, P], F32)
+                tiles["gn", b] = gn
+            nc.scalar.activation(
+                out=tiles["gn", b][:, j, :, :],
+                in_=tiles["norm_t", b, j][:],
+                func=ACT.Identity,
+                scale=gain[:, j : j + 1],
+                bias=shift[:, j : j + 1],
+            )
+
+        def skip_product(b, t):
+            rows = slice(t * P, (t + 1) * P)
+            skip_t = psum_skip.tile([P, GROUPS, P], F32)
+            for j in range(GROUPS):
+                cols = slice(j * P, (j + 1) * P)
+                nc.tensor.matmul_mx(
+                    out=skip_t[:, j, :],
+                    lhsT=skip_codes[:, cols].bitcast(FP8X4),
+                    lhsT_scale=skip_scales[:, cols],
+                    rhs=tiles["xc_codes", b][:, rows].bitcast(FP8X4),
+                    rhs_scale=tiles["xc_scales", b][:, rows],
+                    start=True,
+                    stop=True,
+                )
+            tiles["skip_t", b, t] = skip_t
+
+        def add_streams(b, t):
+            summed = work.tile([P, P, GROUPS], F32, bufs=3)
             nc.vector.tensor_tensor(
-                out=g_grouped[:],
-                in0=summed[:].rearrange("p t r j -> p (t r j)"),
-                in1=gate[:].rearrange("p t r j -> p (t r j)"),
+                out=summed[:],
+                in0=tiles["skip_t", b, t][:].rearrange("p j r -> p r j"),
+                in1=tiles["gn", b][:, :, t, :].rearrange("p j r -> p r j"),
+                op=ALU.add,
+            )
+            tiles["summed", b, t] = summed
+
+        def apply_gate(b, t):
+            if t == 0:
+                g_grouped = work.tile([P, TILES, P, GROUPS], BF16, align_bytes=64)
+                tiles["g_grouped", b] = g_grouped
+            nc.vector.tensor_tensor(
+                out=tiles["g_grouped", b][:, t, :, :],
+                in0=tiles["summed", b, t][:],
+                in1=tiles["gate", b][:, t, :, :],
                 op=ALU.mult,
             )
+
+        def quantise_g(b):
             g_codes = work.tile([P, TILES * P], U32, align_bytes=64)
             g_scales = work.tile([P, TILES * P], U8, align_bytes=64)
-            quantise(nc, g_codes[:], g_scales[:], g_grouped[:])
+            quantise(nc, g_codes[:], g_scales[:], tiles["g_grouped", b][:].rearrange("p t r j -> p (t r j)"))
+            tiles["g_codes", b], tiles["g_scales", b] = g_codes, g_scales
 
-            y = psum_y.tile([P, TILES, IN], F32)
+        def down_product(b):
+            y = psum_misc.tile([P, TILES, IN], F32, tag="misc")
             for t in range(TILES):
                 rows = slice(t * P, (t + 1) * P)
                 nc.tensor.matmul_mx(
                     out=y[:, t, :],
-                    lhsT=g_codes[:, rows].bitcast(FP8X4),
-                    lhsT_scale=g_scales[:, rows],
+                    lhsT=tiles["g_codes", b][:, rows].bitcast(FP8X4),
+                    lhsT_scale=tiles["g_scales", b][:, rows],
                     rhs=down_codes[:].bitcast(FP8X4),
                     rhs_scale=down_scales[:],
                     start=True,
                     stop=True,
                 )
-            residual = work.tile([P, TILES, IN], F32)
-            nc.gpsimd.tensor_tensor(
-                out=residual[:],
-                in0=x_blk[:],
-                in1=down_b_all[:].unsqueeze(1).to_broadcast([P, TILES, IN]),
-                op=ALU.add,
-            )
+            tiles["y", b] = y
+
+        def add_residual_and_store(b):
             result = work.tile([P, TILES, IN], F32)
-            nc.vector.tensor_tensor(out=result[:], in0=y[:], in1=residual[:], op=ALU.add)
+            nc.vector.tensor_tensor(out=result[:], in0=tiles["y", b][:], in1=tiles["residual", b][:], op=ALU.add)
             nc.sync.dma_start(out=out_blocks[b], in_=result[:])
+
+        def run(piece, b, *part):
+            if 0 <= b < N_BLOCKS:
+                piece(b, *part)
+
+        with tc.manual_schedule():
+            for i in range(-4, N_BLOCKS + 2):
+                run(load_h_and_x, i + 4)
+                run(load_x_conv_and_x_right, i + 3)
+                for s in range(TILES):
+                    half = s % 2
+                    if s == 2:
+                        run(down_product, i - 2)
+                    run(skip_product, i - 1, s)
+                    run(transpose_norm, i, s)
+                    if s < 2:
+                        run(transpose_x_conv, i + 1, half)
+                    else:
+                        run(transpose_x_right, i + 1, half)
+                    run(normalise, i + 1, s)
+                    run(gain_and_biases, i, s)
+                    if s < 2:
+                        run(group_x_conv, i + 1, half)
+                    else:
+                        run(silu_gate, i + 1, half)
+                    run(add_streams, i - 1, s)
+                    if s < 2:
+                        run(group_stats, i + 3, 2 * s)
+                        run(group_stats, i + 3, 2 * s + 1)
+                    if s == 2:
+                        run(join_halves_sums, i + 3)
+                    if s == 3:
+                        run(quantise_x_conv, i + 1)
+                        run(join_halves_variance, i + 3)
+                    run(apply_gate, i - 1, s)
+                    if s == 2:
+                        run(join_halves_between, i + 3)
+                    if s == 3:
+                        run(add_residual_and_store, i - 2)
+                        run(quantise_g, i - 1)
+                run(rstd_and_residual, i + 3)

@@ -274,9 +274,9 @@ def tile_mlstmblock_pc_t_kernel(
         def add_streams(b, t):
             summed = work.tile([P, P, GROUPS], F32, bufs=3)
             nc.vector.tensor_tensor(
-                out=summed[:],
-                in0=tiles["skip_t", b, t][:].rearrange("p j r -> p r j"),
-                in1=tiles["gn", b][:, :, t, :].rearrange("p j r -> p r j"),
+                out=summed[:].rearrange("p (c i) j -> p c j i", i=4),
+                in0=tiles["skip_t", b, t][:].rearrange("p j (c i) -> p c j i", i=4),
+                in1=tiles["gn", b][:, :, t, :].rearrange("p j (c i) -> p c j i", i=4),
                 op=ALU.add,
             )
             tiles["summed", b, t] = summed

@@ -20,7 +20,8 @@ EPS = 1e-5
 TILES = 4
 BLOCK = TILES * P
 N_BLOCKS = B // BLOCK
-HALF = TILES // 2
+PAIR = 2
+LINE = 4
 
 FLOPS = 2 * B * PROJ * HID + 2 * B * HID * IN
 
@@ -43,134 +44,99 @@ def tile_mlstmblock_pc_t_kernel(
         consts = ctx.enter_context(tc.tile_pool(name="consts", bufs=1))
         loads = ctx.enter_context(tc.tile_pool(name="loads", bufs=3))
         work = ctx.enter_context(tc.tile_pool(name="work", bufs=2))
-        held = ctx.enter_context(tc.tile_pool(name="held", bufs=3))
+        held = ctx.enter_context(tc.tile_pool(name="held", bufs=4))
         small = ctx.enter_context(tc.tile_pool(name="small", bufs=4))
-        psum_xr = ctx.enter_context(tc.psum_pool(name="psum_xr", bufs=2))
-        psum_n = ctx.enter_context(tc.psum_pool(name="psum_n", bufs=2))
+        psum_in = ctx.enter_context(tc.psum_pool(name="psum_in", bufs=3))
+        psum_norm = ctx.enter_context(tc.psum_pool(name="psum_norm", bufs=2))
         psum_skip = ctx.enter_context(tc.psum_pool(name="psum_skip", bufs=2))
-        psum_misc = ctx.enter_context(tc.psum_pool(name="psum_misc", bufs=2))
+        psum_y = ctx.enter_context(tc.psum_pool(name="psum_y", bufs=1))
 
-        ident_bf16 = consts.tile([P, P], BF16)
-        make_identity(nc, ident_bf16[:])
         ident_f32 = consts.tile([P, P], F32)
         make_identity(nc, ident_f32[:])
+        neg_half = consts.tile([P, TILES * GROUPS, 1], F32)
+        nc.vector.memset(neg_half[:], -0.5)
 
         skip_raw = consts.tile([P, PACK, HID], BF16)
+        down_raw = consts.tile([P, PACK, IN], BF16)
         for u in range(2):
             nc.scalar.dma_start(
                 out=skip_raw[:, 2 * u : 2 * u + 2, :],
                 in_=skip_w[256 * u : 256 * u + 256, :].rearrange("(p e) c -> p e c", e=2),
             )
-        skip_grouped = consts.tile([P, HID, PACK], BF16, align_bytes=64)
-        nc.vector.tensor_copy(out=skip_grouped[:], in_=skip_raw[:].rearrange("p k c -> p c k"))
-        skip_codes = consts.tile([P, HID], U32, align_bytes=64)
-        skip_scales = consts.tile([P, HID], U8, align_bytes=64)
-
-        down_raw = consts.tile([P, PACK, IN], BF16)
-        nc.scalar.dma_start(out=down_raw[:], in_=down_w.rearrange("(j p) c -> p j c", p=P))
-        down_grouped = consts.tile([P, IN, PACK], BF16, align_bytes=64)
-        nc.vector.tensor_copy(out=down_grouped[:], in_=down_raw[:].rearrange("p k c -> p c k"))
-        down_codes = consts.tile([P, IN], U32, align_bytes=64)
-        down_scales = consts.tile([P, IN], U8, align_bytes=64)
-        quantise(nc, skip_codes[:], skip_scales[:], skip_grouped[:].rearrange("p c k -> p (c k)"))
-        quantise(nc, down_codes[:], down_scales[:], down_grouped[:].rearrange("p c k -> p (c k)"))
-
-        vec_rows = consts.tile([P, P], BF16)
-        nc.vector.memset(vec_rows[:], 0.0)
-        for i, vec in enumerate((gn_w, gn_b, skip_b)):
-            nc.gpsimd.dma_start(
-                out=vec_rows[GROUPS * i : GROUPS * (i + 1), :], in_=vec.rearrange("(j p) -> j p", p=P)
+            nc.scalar.dma_start(
+                out=down_raw[:, 2 * u : 2 * u + 2, :],
+                in_=down_w[256 * u : 256 * u + 256, :].rearrange("(p e) c -> p e c", e=2),
             )
-        vec_t = psum_xr.tile([P, HALF, GROUPS, P], BF16, tag="xr_t")
-        nc.tensor.transpose(vec_t[:, 0, 0, :], vec_rows[:], ident_bf16[:])
-        vec_cols = consts.tile([P, 3 * GROUPS], F32)
-        nc.vector.tensor_copy(out=vec_cols[:], in_=vec_t[:, 0, 0, 0 : 3 * GROUPS])
-        gain = vec_cols[:, 0:GROUPS]
-        shift = consts.tile([P, GROUPS], F32)
-        nc.vector.tensor_tensor(
-            out=shift[:], in0=vec_cols[:, GROUPS : 2 * GROUPS], in1=vec_cols[:, 2 * GROUPS : 3 * GROUPS], op=ALU.add
-        )
-
+        vec_rows = consts.tile([P, 2 * P], BF16)
+        nc.vector.memset(vec_rows[:], 0.0)
+        for v, vec in enumerate((gn_w, gn_b, skip_b)):
+            nc.gpsimd.dma_start(out=vec_rows[2 * v : 2 * v + 2, :], in_=vec.rearrange("(u c) -> u c", u=2))
         down_b_all = consts.tile([P, IN], BF16)
         nc.gpsimd.dma_start(out=down_b_all[:], in_=down_b.partition_broadcast(P))
-        neg_half = consts.tile([P, TILES * GROUPS, 1], F32)
-        nc.vector.memset(neg_half[:], -0.5)
+
+        skip_codes = consts.tile([P, HID], U32, align_bytes=64)
+        skip_scales = consts.tile([P, HID], U8, align_bytes=64)
+        down_codes = consts.tile([P, IN], U32, align_bytes=64)
+        down_scales = consts.tile([P, IN], U8, align_bytes=64)
+        vec_cols = consts.tile([P, 3 * PACK], F32)
+        gain = vec_cols[:, 0:PACK]
+        shift = consts.tile([P, PACK], F32)
+
+        def prepare_weights():
+            skip_grouped = consts.tile([P, PACK, P, PACK], BF16, align_bytes=64)
+            for u in range(2):
+                nc.vector.tensor_copy(
+                    out=skip_grouped[:, 2 * u : 2 * u + 2, :, :],
+                    in_=skip_raw[:, :, 256 * u : 256 * u + 256].rearrange("p k (m e) -> p e m k", e=2),
+                )
+            down_grouped = consts.tile([P, IN, PACK], BF16, align_bytes=64)
+            nc.vector.tensor_copy(out=down_grouped[:], in_=down_raw[:].rearrange("p k c -> p c k"))
+            quantise(nc, skip_codes[:], skip_scales[:], skip_grouped[:].rearrange("p q m k -> p (q m k)"))
+            quantise(nc, down_codes[:], down_scales[:], down_grouped[:].rearrange("p c k -> p (c k)"))
+            vec_t = psum_in.tile([P, PAIR, 2, P], F32, tag="in_t")
+            nc.tensor.transpose(vec_t[:, 0, 0, :], vec_rows[:].bitcast(F32), ident_f32[:])
+            nc.vector.tensor_copy(out=vec_cols[:], in_=vec_t[:, 0, 0, :].bitcast(BF16)[:, 0 : 3 * PACK])
+            nc.vector.tensor_tensor(
+                out=shift[:], in0=vec_cols[:, PACK : 2 * PACK], in1=vec_cols[:, 2 * PACK : 3 * PACK], op=ALU.add
+            )
 
         tiles = {}
 
-        def load_h_and_x(b):
-            h_blk = loads.tile([P, TILES, HID], BF16, bufs=4)
+        def load(b):
+            h_blk = loads.tile([P, TILES, HID], BF16)
             nc.sync.dma_start(out=h_blk[:], in_=h_blocks[b])
-            x_blk = loads.tile([P, TILES, IN], BF16)
-            nc.sync.dma_start(out=x_blk[:], in_=x_blocks[b])
-            tiles["h", b], tiles["x", b] = h_blk, x_blk
-
-        def load_x_conv_and_x_right(b):
             xc_blk = loads.tile([P, TILES, PROJ], BF16)
             nc.sync.dma_start(out=xc_blk[:], in_=xc_blocks[b])
             xr_blk = loads.tile([P, TILES, HID], BF16)
             nc.sync.dma_start(out=xr_blk[:], in_=xr_blocks[b])
-            tiles["xc", b], tiles["xr", b] = xc_blk, xr_blk
+            x_blk = loads.tile([P, TILES, IN], BF16)
+            nc.sync.dma_start(out=x_blk[:], in_=x_blocks[b])
+            tiles["h", b], tiles["xc", b], tiles["xr", b], tiles["x", b] = h_blk, xc_blk, xr_blk, x_blk
 
-        def group_stats(b, t):
-            if t == 0:
-                stats = small.tile([P, TILES * GROUPS, 6], F32)
-                tiles["stats", b] = stats
-            for j in range(GROUPS):
-                nc.vector.bn_stats(
-                    out=tiles["stats", b][:, t * GROUPS + j, :],
-                    in_=tiles["h", b][:, t, j * GROUP : (j + 1) * GROUP],
-                )
-
-        def join_halves_sums(b):
-            stats = tiles["stats", b]
-            mean_even, m2_even = stats[:, :, 1:2], stats[:, :, 2:3]
-            mean_odd, m2_odd = stats[:, :, 4:5], stats[:, :, 5:6]
-            mean_sum = small.tile([P, TILES * GROUPS, 1], F32)
-            nc.vector.tensor_tensor(out=mean_sum[:], in0=mean_even, in1=mean_odd, op=ALU.add)
-            mean_diff = small.tile([P, TILES * GROUPS, 1], F32)
-            nc.vector.tensor_tensor(out=mean_diff[:], in0=mean_even, in1=mean_odd, op=ALU.subtract)
-            m2_eps = small.tile([P, TILES * GROUPS, 1], F32)
-            nc.vector.scalar_tensor_tensor(
-                out=m2_eps[:], in0=m2_even, scalar=GROUP * EPS, in1=m2_odd, op0=ALU.add, op1=ALU.add
-            )
-            tiles["mean_sum", b], tiles["mean_diff", b], tiles["m2_eps", b] = mean_sum, mean_diff, m2_eps
-
-        def join_halves_between(b):
-            between = small.tile([P, TILES * GROUPS, 1], F32)
-            nc.vector.scalar_tensor_tensor(
-                out=between[:],
-                in0=tiles["mean_diff", b][:],
-                scalar=0.25,
-                in1=tiles["mean_diff", b][:],
-                op0=ALU.mult,
-                op1=ALU.mult,
-            )
-            tiles["between", b] = between
-
-        def join_halves_variance(b):
-            var_eps = small.tile([P, TILES * GROUPS, 1], F32)
-            nc.vector.scalar_tensor_tensor(
-                out=var_eps[:],
-                in0=tiles["m2_eps", b][:],
-                scalar=1.0 / GROUP,
-                in1=tiles["between", b][:],
-                op0=ALU.mult,
-                op1=ALU.add,
-            )
-            tiles["var_eps", b] = var_eps
+        def group_stats(b):
+            stats = small.tile([P, TILES * GROUPS, 3], F32)
+            for t in range(TILES):
+                for two in range(GROUPS // 2):
+                    nc.vector.bn_stats(
+                        out=stats[:, t * GROUPS + 2 * two : t * GROUPS + 2 * two + 2, :].rearrange("p g s -> p (g s)"),
+                        in_=tiles["h", b][:, t, 2 * two * GROUP : (2 * two + 2) * GROUP].rearrange(
+                            "p (g m) -> p m g", g=2
+                        ),
+                    )
+            tiles["stats", b] = stats
 
         def rstd_and_residual(b):
-            rstd = small.tile([P, TILES * GROUPS, 1], F32)
-            nc.gpsimd.tensor_tensor(out=rstd[:], in0=tiles["var_eps", b][:], in1=neg_half[:], op=ALU.pow)
+            mean, m2 = tiles["stats", b][:, :, 1:2], tiles["stats", b][:, :, 2:3]
             neg_mean = small.tile([P, TILES * GROUPS, 1], F32)
-            nc.gpsimd.tensor_scalar(
-                out=neg_mean[:], in0=tiles["mean_sum", b][:], scalar1=-0.5, scalar2=0.0, op0=ALU.mult, op1=ALU.add
-            )
+            nc.gpsimd.tensor_scalar(out=neg_mean[:], in0=mean, scalar1=-1.0, scalar2=0.0, op0=ALU.mult, op1=ALU.add)
+            var_eps = small.tile([P, TILES * GROUPS, 1], F32)
+            nc.gpsimd.tensor_scalar(out=var_eps[:], in0=m2, scalar1=1.0 / GROUP, scalar2=EPS, op0=ALU.mult, op1=ALU.add)
+            rstd = small.tile([P, TILES * GROUPS, 1], F32)
+            nc.gpsimd.tensor_tensor(out=rstd[:], in0=var_eps[:], in1=neg_half[:], op=ALU.pow)
             neg_mean_rstd = small.tile([P, TILES * GROUPS, 1], F32)
             nc.gpsimd.tensor_tensor(out=neg_mean_rstd[:], in0=neg_mean[:], in1=rstd[:], op=ALU.mult)
             tiles["rstd", b], tiles["neg_mean_rstd", b] = rstd, neg_mean_rstd
-            residual = held.tile([P, TILES, IN], F32, bufs=6)
+            residual = held.tile([P, TILES, IN], F32, bufs=5)
             nc.gpsimd.tensor_tensor(
                 out=residual[:],
                 in0=tiles["x", b][:],
@@ -181,87 +147,76 @@ def tile_mlstmblock_pc_t_kernel(
 
         def normalise(b, t):
             if t == 0:
-                norm = work.tile([P, TILES, HID], F32)
+                norm = work.tile([P, TILES, PACK, P], F32)
                 tiles["norm", b] = norm
             for j in range(GROUPS):
-                cols = slice(j * GROUP, (j + 1) * GROUP)
+                u, m0 = j // 2, (j % 2) * (P // 2)
                 nc.scalar.activation(
-                    out=tiles["norm", b][:, t, cols],
-                    in_=tiles["h", b][:, t, cols],
+                    out=tiles["norm", b][:, t, 2 * u : 2 * u + 2, m0 : m0 + P // 2],
+                    in_=tiles["h", b][:, t, j * GROUP : (j + 1) * GROUP].rearrange("p (m e) -> p e m", e=2),
                     func=ACT.Identity,
                     scale=tiles["rstd", b][:, t * GROUPS + j, :],
                     bias=tiles["neg_mean_rstd", b][:, t * GROUPS + j, :],
                 )
 
-        def transpose_x_conv(b, half):
-            xc_words = tiles["xc", b][:].bitcast(F32)
-            xc_t = psum_misc.tile([P, HALF, 2, P], F32, tag="misc")
-            for i in range(HALF):
+        def transpose_words(b, name, pair):
+            words = tiles[name, b][:].bitcast(F32)
+            in_t = psum_in.tile([P, PAIR, 2, P], F32)
+            for i in range(PAIR):
                 for u in range(2):
-                    nc.tensor.transpose(
-                        xc_t[:, i, u, :], xc_words[:, half * HALF + i, u * P : (u + 1) * P], ident_f32[:]
-                    )
-            tiles["xc_t", b, half] = xc_t
+                    nc.tensor.transpose(in_t[:, i, u, :], words[:, pair * PAIR + i, u * P : (u + 1) * P], ident_f32[:])
+            tiles[name + "_t", b, pair] = in_t
 
-        def group_x_conv(b, half):
-            if half == 0:
+        def group_x_conv(b, pair):
+            if pair == 0:
                 xc_grouped = work.tile([P, TILES, P, PACK], BF16, align_bytes=64)
                 tiles["xc_grouped", b] = xc_grouped
             nc.scalar.copy(
-                out=tiles["xc_grouped", b][:].bitcast(F32)[:, half * HALF : (half + 1) * HALF, :, :],
-                in_=tiles["xc_t", b, half][:].rearrange("p i u r -> p i r u"),
+                out=tiles["xc_grouped", b][:].bitcast(F32)[:, pair * PAIR : (pair + 1) * PAIR, :, :],
+                in_=tiles["xc_t", b, pair][:].rearrange("p i u r -> p i r u"),
             )
 
         def quantise_x_conv(b):
             xc_codes = held.tile([P, TILES * P], U32, align_bytes=64)
             xc_scales = held.tile([P, TILES * P], U8, align_bytes=64)
-            quantise(nc, xc_codes[:], xc_scales[:], tiles["xc_grouped", b][:].rearrange("p t r k -> p (t r k)"))
+            quantise(nc, xc_codes[:], xc_scales[:], tiles["xc_grouped", b][:].rearrange("p t r q -> p (t r q)"))
             tiles["xc_codes", b], tiles["xc_scales", b] = xc_codes, xc_scales
 
-        def transpose_x_right(b, half):
-            xr_t = psum_xr.tile([P, HALF, GROUPS, P], BF16)
-            for i in range(HALF):
-                for j in range(GROUPS):
-                    nc.tensor.transpose(
-                        xr_t[:, i, j, :], tiles["xr", b][:, half * HALF + i, j * P : (j + 1) * P], ident_bf16[:]
-                    )
-            tiles["xr_t", b, half] = xr_t
-
-        def silu_gate(b, half):
-            if half == 0:
-                gate = held.tile([P, TILES, P, GROUPS], F32)
+        def silu_gate(b, t):
+            if t == 0:
+                gate = held.tile([P, TILES, P, PACK], F32)
                 tiles["gate", b] = gate
             nc.scalar.activation(
-                out=tiles["gate", b][:, half * HALF : (half + 1) * HALF, :, :],
-                in_=tiles["xr_t", b, half][:].rearrange("p i j r -> p i r j"),
+                out=tiles["gate", b][:, t, :, :].rearrange("p r (u e) -> p r u e", e=2),
+                in_=tiles["xr_t", b, t // PAIR][:, t % PAIR, :, :].bitcast(BF16).rearrange("p u (r e) -> p r u e", e=2),
                 func=ACT.Silu,
             )
 
-        def transpose_norm(b, j):
-            norm_t = psum_n.tile([P, TILES, P], F32)
+        def transpose_norm(b, q):
+            norm_t = psum_norm.tile([P, TILES, P], F32)
             for t in range(TILES):
-                nc.tensor.transpose(norm_t[:, t, :], tiles["norm", b][:, t, j * P : (j + 1) * P], ident_f32[:])
-            tiles["norm_t", b, j] = norm_t
+                nc.tensor.transpose(norm_t[:, t, :], tiles["norm", b][:, t, q, :], ident_f32[:])
+            tiles["norm_t", b, q] = norm_t
 
-        def gain_and_biases(b, j):
-            if j == 0:
-                gn = work.tile([P, GROUPS, TILES, P], F32)
+        def gain_and_biases(b, q):
+            if q == 0:
+                gn = work.tile([P, PACK, TILES, P], F32)
                 tiles["gn", b] = gn
             nc.scalar.activation(
-                out=tiles["gn", b][:, j, :, :],
-                in_=tiles["norm_t", b, j][:],
+                out=tiles["gn", b][:, q, :, :],
+                in_=tiles["norm_t", b, q][:],
                 func=ACT.Identity,
-                scale=gain[:, j : j + 1],
-                bias=shift[:, j : j + 1],
+                scale=gain[:, q : q + 1],
+                bias=shift[:, q : q + 1],
             )
 
         def skip_product(b, t):
             rows = slice(t * P, (t + 1) * P)
-            skip_t = psum_skip.tile([P, GROUPS, P], F32)
-            for j in range(GROUPS):
-                cols = slice(j * P, (j + 1) * P)
+            skip_t = psum_skip.tile([P, PACK, P], F32)
+            for q in range(PACK):
+                cols = slice(q * P, (q + 1) * P)
                 nc.tensor.matmul_mx(
-                    out=skip_t[:, j, :],
+                    out=skip_t[:, q, :],
                     lhsT=skip_codes[:, cols].bitcast(FP8X4),
                     lhsT_scale=skip_scales[:, cols],
                     rhs=tiles["xc_codes", b][:, rows].bitcast(FP8X4),
@@ -272,18 +227,18 @@ def tile_mlstmblock_pc_t_kernel(
             tiles["skip_t", b, t] = skip_t
 
         def add_streams(b, t):
-            summed = work.tile([P, P, GROUPS], F32, bufs=3)
+            summed = work.tile([P, P, PACK], F32, bufs=4)
             nc.vector.tensor_tensor(
-                out=summed[:].rearrange("p (c i) j -> p c j i", i=4),
-                in0=tiles["skip_t", b, t][:].rearrange("p j (c i) -> p c j i", i=4),
-                in1=tiles["gn", b][:, :, t, :].rearrange("p j (c i) -> p c j i", i=4),
+                out=summed[:].rearrange("p (c i) q -> p c q i", i=LINE),
+                in0=tiles["skip_t", b, t][:].rearrange("p q (c i) -> p c q i", i=LINE),
+                in1=tiles["gn", b][:, :, t, :].rearrange("p q (c i) -> p c q i", i=LINE),
                 op=ALU.add,
             )
             tiles["summed", b, t] = summed
 
         def apply_gate(b, t):
             if t == 0:
-                g_grouped = work.tile([P, TILES, P, GROUPS], BF16, align_bytes=64)
+                g_grouped = work.tile([P, TILES, P, PACK], BF16, align_bytes=64)
                 tiles["g_grouped", b] = g_grouped
             nc.vector.tensor_tensor(
                 out=tiles["g_grouped", b][:, t, :, :],
@@ -295,11 +250,11 @@ def tile_mlstmblock_pc_t_kernel(
         def quantise_g(b):
             g_codes = work.tile([P, TILES * P], U32, align_bytes=64)
             g_scales = work.tile([P, TILES * P], U8, align_bytes=64)
-            quantise(nc, g_codes[:], g_scales[:], tiles["g_grouped", b][:].rearrange("p t r j -> p (t r j)"))
+            quantise(nc, g_codes[:], g_scales[:], tiles["g_grouped", b][:].rearrange("p t r q -> p (t r q)"))
             tiles["g_codes", b], tiles["g_scales", b] = g_codes, g_scales
 
         def down_product(b):
-            y = psum_misc.tile([P, TILES, IN], F32, tag="misc")
+            y = psum_y.tile([P, TILES, IN], F32)
             for t in range(TILES):
                 rows = slice(t * P, (t + 1) * P)
                 nc.tensor.matmul_mx(
@@ -322,39 +277,52 @@ def tile_mlstmblock_pc_t_kernel(
             if 0 <= b < N_BLOCKS:
                 piece(b, *part)
 
+        def turn(i):
+            run(load, i + 3)
+            run(skip_product, i - 1, 0)
+            run(skip_product, i - 1, 1)
+            run(transpose_words, i + 2, "xc", 0)
+            run(transpose_words, i + 2, "xc", 1)
+            run(transpose_norm, i, 0)
+            run(transpose_norm, i, 1)
+            run(group_x_conv, i + 2, 0)
+            run(group_x_conv, i + 2, 1)
+            run(gain_and_biases, i, 0)
+            run(gain_and_biases, i, 1)
+            run(normalise, i + 1, 0)
+            run(normalise, i + 1, 1)
+            run(add_streams, i - 1, 0)
+            run(add_streams, i - 1, 1)
+            run(group_stats, i + 2)
+            run(rstd_and_residual, i + 2)
+            run(down_product, i - 2)
+            run(skip_product, i - 1, 2)
+            run(skip_product, i - 1, 3)
+            run(transpose_words, i + 2, "xr", 0)
+            run(transpose_words, i + 2, "xr", 1)
+            run(transpose_norm, i, 2)
+            run(transpose_norm, i, 3)
+            run(silu_gate, i + 2, 0)
+            run(silu_gate, i + 2, 1)
+            run(gain_and_biases, i, 2)
+            run(silu_gate, i + 2, 2)
+            run(silu_gate, i + 2, 3)
+            run(gain_and_biases, i, 3)
+            run(normalise, i + 1, 2)
+            run(normalise, i + 1, 3)
+            run(add_streams, i - 1, 2)
+            run(add_streams, i - 1, 3)
+            run(apply_gate, i - 1, 0)
+            run(apply_gate, i - 1, 1)
+            run(quantise_x_conv, i + 2)
+            run(apply_gate, i - 1, 2)
+            run(apply_gate, i - 1, 3)
+            run(add_residual_and_store, i - 2)
+            run(quantise_g, i - 1)
+
         with tc.manual_schedule():
-            for i in range(-4, N_BLOCKS + 2):
-                run(load_h_and_x, i + 4)
-                run(load_x_conv_and_x_right, i + 3)
-                for s in range(TILES):
-                    half = s % 2
-                    if s == 2:
-                        run(down_product, i - 2)
-                    run(skip_product, i - 1, s)
-                    run(transpose_norm, i, s)
-                    if s < 2:
-                        run(transpose_x_conv, i + 1, half)
-                    else:
-                        run(transpose_x_right, i + 1, half)
-                    run(normalise, i + 1, s)
-                    run(gain_and_biases, i, s)
-                    if s < 2:
-                        run(group_x_conv, i + 1, half)
-                    else:
-                        run(silu_gate, i + 1, half)
-                    run(add_streams, i - 1, s)
-                    if s < 2:
-                        run(group_stats, i + 3, 2 * s)
-                        run(group_stats, i + 3, 2 * s + 1)
-                    if s == 2:
-                        run(join_halves_sums, i + 3)
-                    if s == 3:
-                        run(quantise_x_conv, i + 1)
-                        run(join_halves_variance, i + 3)
-                    run(apply_gate, i - 1, s)
-                    if s == 2:
-                        run(join_halves_between, i + 3)
-                    if s == 3:
-                        run(add_residual_and_store, i - 2)
-                        run(quantise_g, i - 1)
-                run(rstd_and_residual, i + 3)
+            turn(-3)
+            turn(-2)
+            prepare_weights()
+            for i in range(-1, N_BLOCKS + 2):
+                turn(i)

@@ -46,9 +46,9 @@ def tile_mlstmblock_pc_t_kernel(
         work = ctx.enter_context(tc.tile_pool(name="work", bufs=2))
         held = ctx.enter_context(tc.tile_pool(name="held", bufs=4))
         small = ctx.enter_context(tc.tile_pool(name="small", bufs=4))
-        psum_in = ctx.enter_context(tc.psum_pool(name="psum_in", bufs=3))
+        psum_in = ctx.enter_context(tc.psum_pool(name="psum_in", bufs=2))
         psum_norm = ctx.enter_context(tc.psum_pool(name="psum_norm", bufs=2))
-        psum_skip = ctx.enter_context(tc.psum_pool(name="psum_skip", bufs=2))
+        psum_skip = ctx.enter_context(tc.psum_pool(name="psum_skip", bufs=3))
         psum_y = ctx.enter_context(tc.psum_pool(name="psum_y", bufs=1))
 
         ident_f32 = consts.tile([P, P], F32)
@@ -279,8 +279,6 @@ def tile_mlstmblock_pc_t_kernel(
 
         def turn(i):
             run(load, i + 3)
-            run(skip_product, i - 1, 0)
-            run(skip_product, i - 1, 1)
             run(transpose_words, i + 2, "xc", 0)
             run(transpose_words, i + 2, "xc", 1)
             run(transpose_norm, i, 0)
@@ -289,31 +287,29 @@ def tile_mlstmblock_pc_t_kernel(
             run(group_x_conv, i + 2, 1)
             run(gain_and_biases, i, 0)
             run(gain_and_biases, i, 1)
-            run(normalise, i + 1, 0)
-            run(normalise, i + 1, 1)
-            run(add_streams, i - 1, 0)
-            run(add_streams, i - 1, 1)
-            run(group_stats, i + 2)
-            run(rstd_and_residual, i + 2)
-            run(down_product, i - 2)
-            run(skip_product, i - 1, 2)
-            run(skip_product, i - 1, 3)
-            run(transpose_words, i + 2, "xr", 0)
-            run(transpose_words, i + 2, "xr", 1)
             run(transpose_norm, i, 2)
             run(transpose_norm, i, 3)
-            run(silu_gate, i + 2, 0)
-            run(silu_gate, i + 2, 1)
+            run(transpose_words, i + 2, "xr", 0)
+            run(transpose_words, i + 2, "xr", 1)
             run(gain_and_biases, i, 2)
-            run(silu_gate, i + 2, 2)
-            run(silu_gate, i + 2, 3)
             run(gain_and_biases, i, 3)
-            run(normalise, i + 1, 2)
-            run(normalise, i + 1, 3)
+            for t in range(TILES):
+                run(silu_gate, i + 2, t)
+            for t in range(TILES):
+                run(normalise, i + 1, t)
+            run(add_streams, i - 1, 0)
+            run(down_product, i - 2)
+            run(skip_product, i - 1, 3)
+            run(add_streams, i - 1, 1)
+            run(skip_product, i, 0)
+            run(group_stats, i + 2)
+            run(rstd_and_residual, i + 2)
             run(add_streams, i - 1, 2)
-            run(add_streams, i - 1, 3)
+            run(skip_product, i, 1)
             run(apply_gate, i - 1, 0)
             run(apply_gate, i - 1, 1)
+            run(add_streams, i - 1, 3)
+            run(skip_product, i, 2)
             run(quantise_x_conv, i + 2)
             run(apply_gate, i - 1, 2)
             run(apply_gate, i - 1, 3)

@@ -17,10 +17,9 @@ B, IN, HID, PROJ = 8192, 128, 512, 512
 GROUPS = 4
 GROUP = HID // GROUPS
 EPS = 1e-5
-TILES = 4
+TILES = 2
 BLOCK = TILES * P
 N_BLOCKS = B // BLOCK
-PAIR = 2
 LINE = 4
 
 FLOPS = 2 * B * PROJ * HID + 2 * B * HID * IN
@@ -46,9 +45,9 @@ def tile_mlstmblock_pc_t_kernel(
         work = ctx.enter_context(tc.tile_pool(name="work", bufs=2))
         held = ctx.enter_context(tc.tile_pool(name="held", bufs=4))
         small = ctx.enter_context(tc.tile_pool(name="small", bufs=4))
-        psum_in = ctx.enter_context(tc.psum_pool(name="psum_in", bufs=2))
+        psum_in = ctx.enter_context(tc.psum_pool(name="psum_in", bufs=3))
         psum_norm = ctx.enter_context(tc.psum_pool(name="psum_norm", bufs=2))
-        psum_skip = ctx.enter_context(tc.psum_pool(name="psum_skip", bufs=3))
+        psum_skip = ctx.enter_context(tc.psum_pool(name="psum_skip", bufs=2))
         psum_y = ctx.enter_context(tc.psum_pool(name="psum_y", bufs=1))
 
         ident_f32 = consts.tile([P, P], F32)
@@ -93,7 +92,7 @@ def tile_mlstmblock_pc_t_kernel(
             nc.vector.tensor_copy(out=down_grouped[:], in_=down_raw[:].rearrange("p k c -> p c k"))
             quantise(nc, skip_codes[:], skip_scales[:], skip_grouped[:].rearrange("p q m k -> p (q m k)"))
             quantise(nc, down_codes[:], down_scales[:], down_grouped[:].rearrange("p c k -> p (c k)"))
-            vec_t = psum_in.tile([P, PAIR, 2, P], F32, tag="in_t")
+            vec_t = psum_in.tile([P, TILES, 2, P], F32, tag="in_t")
             nc.tensor.transpose(vec_t[:, 0, 0, :], vec_rows[:].bitcast(F32), ident_f32[:])
             nc.vector.tensor_copy(out=vec_cols[:], in_=vec_t[:, 0, 0, :].bitcast(BF16)[:, 0 : 3 * PACK])
             nc.vector.tensor_tensor(
@@ -159,22 +158,18 @@ def tile_mlstmblock_pc_t_kernel(
                     bias=tiles["neg_mean_rstd", b][:, t * GROUPS + j, :],
                 )
 
-        def transpose_words(b, name, pair):
+        def transpose_words(b, name):
             words = tiles[name, b][:].bitcast(F32)
-            in_t = psum_in.tile([P, PAIR, 2, P], F32)
-            for i in range(PAIR):
+            in_t = psum_in.tile([P, TILES, 2, P], F32)
+            for t in range(TILES):
                 for u in range(2):
-                    nc.tensor.transpose(in_t[:, i, u, :], words[:, pair * PAIR + i, u * P : (u + 1) * P], ident_f32[:])
-            tiles[name + "_t", b, pair] = in_t
+                    nc.tensor.transpose(in_t[:, t, u, :], words[:, t, u * P : (u + 1) * P], ident_f32[:])
+            tiles[name + "_t", b] = in_t
 
-        def group_x_conv(b, pair):
-            if pair == 0:
-                xc_grouped = work.tile([P, TILES, P, PACK], BF16, align_bytes=64)
-                tiles["xc_grouped", b] = xc_grouped
-            nc.scalar.copy(
-                out=tiles["xc_grouped", b][:].bitcast(F32)[:, pair * PAIR : (pair + 1) * PAIR, :, :],
-                in_=tiles["xc_t", b, pair][:].rearrange("p i u r -> p i r u"),
-            )
+        def group_x_conv(b):
+            xc_grouped = work.tile([P, TILES, P, PACK], BF16, align_bytes=64)
+            nc.scalar.copy(out=xc_grouped[:].bitcast(F32), in_=tiles["xc_t", b][:].rearrange("p t u r -> p t r u"))
+            tiles["xc_grouped", b] = xc_grouped
 
         def quantise_x_conv(b):
             xc_codes = held.tile([P, TILES * P], U32, align_bytes=64)
@@ -188,15 +183,16 @@ def tile_mlstmblock_pc_t_kernel(
                 tiles["gate", b] = gate
             nc.scalar.activation(
                 out=tiles["gate", b][:, t, :, :].rearrange("p r (u e) -> p r u e", e=2),
-                in_=tiles["xr_t", b, t // PAIR][:, t % PAIR, :, :].bitcast(BF16).rearrange("p u (r e) -> p r u e", e=2),
+                in_=tiles["xr_t", b][:, t, :, :].bitcast(BF16).rearrange("p u (r e) -> p r u e", e=2),
                 func=ACT.Silu,
             )
 
-        def transpose_norm(b, q):
-            norm_t = psum_norm.tile([P, TILES, P], F32)
-            for t in range(TILES):
-                nc.tensor.transpose(norm_t[:, t, :], tiles["norm", b][:, t, q, :], ident_f32[:])
-            tiles["norm_t", b, q] = norm_t
+        def transpose_norm(b, u):
+            norm_t = psum_norm.tile([P, 2, TILES, P], F32)
+            for e in range(2):
+                for t in range(TILES):
+                    nc.tensor.transpose(norm_t[:, e, t, :], tiles["norm", b][:, t, 2 * u + e, :], ident_f32[:])
+            tiles["norm_t", b, u] = norm_t
 
         def gain_and_biases(b, q):
             if q == 0:
@@ -204,7 +200,7 @@ def tile_mlstmblock_pc_t_kernel(
                 tiles["gn", b] = gn
             nc.scalar.activation(
                 out=tiles["gn", b][:, q, :, :],
-                in_=tiles["norm_t", b, q][:],
+                in_=tiles["norm_t", b, q // 2][:, q % 2, :, :],
                 func=ACT.Identity,
                 scale=gain[:, q : q + 1],
                 bias=shift[:, q : q + 1],
@@ -227,25 +223,20 @@ def tile_mlstmblock_pc_t_kernel(
             tiles["skip_t", b, t] = skip_t
 
         def add_streams(b, t):
-            summed = work.tile([P, P, PACK], F32, bufs=4)
+            if t == 0:
+                summed = work.tile([P, TILES, P, PACK], F32)
+                tiles["summed", b] = summed
             nc.vector.tensor_tensor(
-                out=summed[:].rearrange("p (c i) q -> p c q i", i=LINE),
+                out=tiles["summed", b][:, t, :, :].rearrange("p (c i) q -> p c q i", i=LINE),
                 in0=tiles["skip_t", b, t][:].rearrange("p q (c i) -> p c q i", i=LINE),
                 in1=tiles["gn", b][:, :, t, :].rearrange("p q (c i) -> p c q i", i=LINE),
                 op=ALU.add,
             )
-            tiles["summed", b, t] = summed
 
-        def apply_gate(b, t):
-            if t == 0:
-                g_grouped = work.tile([P, TILES, P, PACK], BF16, align_bytes=64)
-                tiles["g_grouped", b] = g_grouped
-            nc.vector.tensor_tensor(
-                out=tiles["g_grouped", b][:, t, :, :],
-                in0=tiles["summed", b, t][:],
-                in1=tiles["gate", b][:, t, :, :],
-                op=ALU.mult,
-            )
+        def apply_gate(b):
+            g_grouped = work.tile([P, TILES, P, PACK], BF16, align_bytes=64)
+            nc.vector.tensor_tensor(out=g_grouped[:], in0=tiles["summed", b][:], in1=tiles["gate", b][:], op=ALU.mult)
+            tiles["g_grouped", b] = g_grouped
 
         def quantise_g(b):
             g_codes = work.tile([P, TILES * P], U32, align_bytes=64)
@@ -279,41 +270,27 @@ def tile_mlstmblock_pc_t_kernel(
 
         def turn(i):
             run(load, i + 3)
-            run(transpose_words, i + 2, "xc", 0)
-            run(transpose_words, i + 2, "xc", 1)
+            run(skip_product, i - 1, 0)
+            run(skip_product, i - 1, 1)
+            run(transpose_words, i + 2, "xc")
+            run(transpose_words, i + 2, "xr")
             run(transpose_norm, i, 0)
             run(transpose_norm, i, 1)
-            run(group_x_conv, i + 2, 0)
-            run(group_x_conv, i + 2, 1)
-            run(gain_and_biases, i, 0)
-            run(gain_and_biases, i, 1)
-            run(transpose_norm, i, 2)
-            run(transpose_norm, i, 3)
-            run(transpose_words, i + 2, "xr", 0)
-            run(transpose_words, i + 2, "xr", 1)
-            run(gain_and_biases, i, 2)
-            run(gain_and_biases, i, 3)
+            run(down_product, i - 2)
+            run(group_x_conv, i + 2)
             for t in range(TILES):
                 run(silu_gate, i + 2, t)
+            for q in range(PACK):
+                run(gain_and_biases, i, q)
             for t in range(TILES):
                 run(normalise, i + 1, t)
-            run(add_streams, i - 1, 0)
-            run(down_product, i - 2)
-            run(skip_product, i - 1, 3)
-            run(add_streams, i - 1, 1)
-            run(skip_product, i, 0)
             run(group_stats, i + 2)
             run(rstd_and_residual, i + 2)
-            run(add_streams, i - 1, 2)
-            run(skip_product, i, 1)
-            run(apply_gate, i - 1, 0)
-            run(apply_gate, i - 1, 1)
-            run(add_streams, i - 1, 3)
-            run(skip_product, i, 2)
-            run(quantise_x_conv, i + 2)
-            run(apply_gate, i - 1, 2)
-            run(apply_gate, i - 1, 3)
+            run(add_streams, i - 1, 0)
+            run(add_streams, i - 1, 1)
             run(add_residual_and_store, i - 2)
+            run(apply_gate, i - 1)
+            run(quantise_x_conv, i + 2)
             run(quantise_g, i - 1)
 
         with tc.manual_schedule():

from contextlib import ExitStack

import concourse.mybir as mybir
from concourse.masks import make_identity

F32 = mybir.dt.float32
BF16 = mybir.dt.bfloat16
U32 = mybir.dt.uint32
U8 = mybir.dt.uint8
FP8X4 = mybir.dt.float8_e4m3fn_x4
ALU = mybir.AluOpType
ACT = mybir.ActivationFunctionType

P = 128
PACK = 4
B, IN, HID, PROJ = 8192, 128, 512, 512
GROUPS = 4
GROUP = HID // GROUPS
EPS = 1e-5
TILES = 2
BLOCK = TILES * P
N_BLOCKS = B // BLOCK
LINE = 4

FLOPS = 2 * B * PROJ * HID + 2 * B * HID * IN


def quantise(nc, codes, scales, grouped):
    nc.vector.quantize_mx(out=codes.bitcast(FP8X4), scales=scales, in_=grouped)


def tile_mlstmblock_pc_t_kernel(
    tc, h_t, x_conv, x_right, x, gn_w, gn_b, skip_w, skip_b, down_w, down_b, out
):
    nc = tc.nc
    h_blocks = h_t.rearrange("(b p t) c -> b p t c", p=P, t=TILES)
    xc_blocks = x_conv.rearrange("(b p t) c -> b p t c", p=P, t=TILES)
    xr_blocks = x_right.rearrange("(b p t) c -> b p t c", p=P, t=TILES)
    x_blocks = x.rearrange("(b p t) c -> b p t c", p=P, t=TILES)
    out_blocks = out.rearrange("(b p t) c -> b p t c", p=P, t=TILES)

    with ExitStack() as ctx:
        consts = ctx.enter_context(tc.tile_pool(name="consts", bufs=1))
        loads = ctx.enter_context(tc.tile_pool(name="loads", bufs=3))
        work = ctx.enter_context(tc.tile_pool(name="work", bufs=2))
        held = ctx.enter_context(tc.tile_pool(name="held", bufs=4))
        small = ctx.enter_context(tc.tile_pool(name="small", bufs=4))
        psum_in = ctx.enter_context(tc.psum_pool(name="psum_in", bufs=3))
        psum_norm = ctx.enter_context(tc.psum_pool(name="psum_norm", bufs=2))
        psum_skip = ctx.enter_context(tc.psum_pool(name="psum_skip", bufs=2))
        psum_y = ctx.enter_context(tc.psum_pool(name="psum_y", bufs=1))

        ident_f32 = consts.tile([P, P], F32)
        make_identity(nc, ident_f32[:])
        neg_half = consts.tile([P, TILES * GROUPS, 1], F32)
        nc.vector.memset(neg_half[:], -0.5)

        skip_raw = consts.tile([P, PACK, HID], BF16)
        down_raw = consts.tile([P, PACK, IN], BF16)
        for u in range(2):
            nc.scalar.dma_start(
                out=skip_raw[:, 2 * u : 2 * u + 2, :],
                in_=skip_w[256 * u : 256 * u + 256, :].rearrange("(p e) c -> p e c", e=2),
            )
            nc.scalar.dma_start(
                out=down_raw[:, 2 * u : 2 * u + 2, :],
                in_=down_w[256 * u : 256 * u + 256, :].rearrange("(p e) c -> p e c", e=2),
            )
        vec_rows = consts.tile([P, 2 * P], BF16)
        nc.vector.memset(vec_rows[:], 0.0)
        for v, vec in enumerate((gn_w, gn_b, skip_b)):
            nc.gpsimd.dma_start(out=vec_rows[2 * v : 2 * v + 2, :], in_=vec.rearrange("(u c) -> u c", u=2))
        down_b_all = consts.tile([P, IN], BF16)
        nc.gpsimd.dma_start(out=down_b_all[:], in_=down_b.partition_broadcast(P))

        skip_codes = consts.tile([P, HID], U32, align_bytes=64)
        skip_scales = consts.tile([P, HID], U8, align_bytes=64)
        down_codes = consts.tile([P, IN], U32, align_bytes=64)
        down_scales = consts.tile([P, IN], U8, align_bytes=64)
        vec_cols = consts.tile([P, 3 * PACK], F32)
        gain = vec_cols[:, 0:PACK]
        shift = consts.tile([P, PACK], F32)

        def prepare_weights():
            skip_grouped = consts.tile([P, PACK, P, PACK], BF16, align_bytes=64)
            for u in range(2):
                nc.vector.tensor_copy(
                    out=skip_grouped[:, 2 * u : 2 * u + 2, :, :],
                    in_=skip_raw[:, :, 256 * u : 256 * u + 256].rearrange("p k (m e) -> p e m k", e=2),
                )
            down_grouped = consts.tile([P, IN, PACK], BF16, align_bytes=64)
            nc.vector.tensor_copy(out=down_grouped[:], in_=down_raw[:].rearrange("p k c -> p c k"))
            quantise(nc, skip_codes[:], skip_scales[:], skip_grouped[:].rearrange("p q m k -> p (q m k)"))
            quantise(nc, down_codes[:], down_scales[:], down_grouped[:].rearrange("p c k -> p (c k)"))
            vec_t = psum_in.tile([P, TILES, 2, P], F32, tag="in_t")
            nc.tensor.transpose(vec_t[:, 0, 0, :], vec_rows[:].bitcast(F32), ident_f32[:])
            nc.vector.tensor_copy(out=vec_cols[:], in_=vec_t[:, 0, 0, :].bitcast(BF16)[:, 0 : 3 * PACK])
            nc.vector.tensor_tensor(
                out=shift[:], in0=vec_cols[:, PACK : 2 * PACK], in1=vec_cols[:, 2 * PACK : 3 * PACK], op=ALU.add
            )

        tiles = {}

        def load(b):
            h_blk = loads.tile([P, TILES, HID], BF16)
            nc.sync.dma_start(out=h_blk[:], in_=h_blocks[b])
            xc_blk = loads.tile([P, TILES, PROJ], BF16)
            nc.sync.dma_start(out=xc_blk[:], in_=xc_blocks[b])
            xr_blk = loads.tile([P, TILES, HID], BF16)
            nc.sync.dma_start(out=xr_blk[:], in_=xr_blocks[b])
            x_blk = loads.tile([P, TILES, IN], BF16)
            nc.sync.dma_start(out=x_blk[:], in_=x_blocks[b])
            tiles["h", b], tiles["xc", b], tiles["xr", b], tiles["x", b] = h_blk, xc_blk, xr_blk, x_blk

        def group_stats(b):
            stats = small.tile([P, TILES * GROUPS, 3], F32)
            for t in range(TILES):
                for two in range(GROUPS // 2):
                    nc.vector.bn_stats(
                        out=stats[:, t * GROUPS + 2 * two : t * GROUPS + 2 * two + 2, :].rearrange("p g s -> p (g s)"),
                        in_=tiles["h", b][:, t, 2 * two * GROUP : (2 * two + 2) * GROUP].rearrange(
                            "p (g m) -> p m g", g=2
                        ),
                    )
            tiles["stats", b] = stats

        def rstd_and_residual(b):
            mean, m2 = tiles["stats", b][:, :, 1:2], tiles["stats", b][:, :, 2:3]
            neg_mean = small.tile([P, TILES * GROUPS, 1], F32)
            nc.gpsimd.tensor_scalar(out=neg_mean[:], in0=mean, scalar1=-1.0, scalar2=0.0, op0=ALU.mult, op1=ALU.add)
            var_eps = small.tile([P, TILES * GROUPS, 1], F32)
            nc.gpsimd.tensor_scalar(out=var_eps[:], in0=m2, scalar1=1.0 / GROUP, scalar2=EPS, op0=ALU.mult, op1=ALU.add)
            rstd = small.tile([P, TILES * GROUPS, 1], F32)
            nc.gpsimd.tensor_tensor(out=rstd[:], in0=var_eps[:], in1=neg_half[:], op=ALU.pow)
            neg_mean_rstd = small.tile([P, TILES * GROUPS, 1], F32)
            nc.gpsimd.tensor_tensor(out=neg_mean_rstd[:], in0=neg_mean[:], in1=rstd[:], op=ALU.mult)
            tiles["rstd", b], tiles["neg_mean_rstd", b] = rstd, neg_mean_rstd
            residual = held.tile([P, TILES, IN], F32, bufs=5)
            nc.gpsimd.tensor_tensor(
                out=residual[:],
                in0=tiles["x", b][:],
                in1=down_b_all[:].unsqueeze(1).to_broadcast([P, TILES, IN]),
                op=ALU.add,
            )
            tiles["residual", b] = residual

        def normalise(b, t):
            if t == 0:
                norm = work.tile([P, TILES, PACK, P], F32)
                tiles["norm", b] = norm
            for j in range(GROUPS):
                u, m0 = j // 2, (j % 2) * (P // 2)
                nc.scalar.activation(
                    out=tiles["norm", b][:, t, 2 * u : 2 * u + 2, m0 : m0 + P // 2],
                    in_=tiles["h", b][:, t, j * GROUP : (j + 1) * GROUP].rearrange("p (m e) -> p e m", e=2),
                    func=ACT.Identity,
                    scale=tiles["rstd", b][:, t * GROUPS + j, :],
                    bias=tiles["neg_mean_rstd", b][:, t * GROUPS + j, :],
                )

        def transpose_words(b, name):
            words = tiles[name, b][:].bitcast(F32)
            in_t = psum_in.tile([P, TILES, 2, P], F32)
            for t in range(TILES):
                for u in range(2):
                    nc.tensor.transpose(in_t[:, t, u, :], words[:, t, u * P : (u + 1) * P], ident_f32[:])
            tiles[name + "_t", b] = in_t

        def group_x_conv(b):
            xc_grouped = work.tile([P, TILES, P, PACK], BF16, align_bytes=64)
            nc.scalar.copy(out=xc_grouped[:].bitcast(F32), in_=tiles["xc_t", b][:].rearrange("p t u r -> p t r u"))
            tiles["xc_grouped", b] = xc_grouped

        def quantise_x_conv(b):
            xc_codes = held.tile([P, TILES * P], U32, align_bytes=64)
            xc_scales = held.tile([P, TILES * P], U8, align_bytes=64)
            quantise(nc, xc_codes[:], xc_scales[:], tiles["xc_grouped", b][:].rearrange("p t r q -> p (t r q)"))
            tiles["xc_codes", b], tiles["xc_scales", b] = xc_codes, xc_scales

        def silu_gate(b, t):
            if t == 0:
                gate = held.tile([P, TILES, P, PACK], F32)
                tiles["gate", b] = gate
            nc.scalar.activation(
                out=tiles["gate", b][:, t, :, :].rearrange("p r (u e) -> p r u e", e=2),
                in_=tiles["xr_t", b][:, t, :, :].bitcast(BF16).rearrange("p u (r e) -> p r u e", e=2),
                func=ACT.Silu,
            )

        def transpose_norm(b, u):
            norm_t = psum_norm.tile([P, 2, TILES, P], F32)
            for e in range(2):
                for t in range(TILES):
                    nc.tensor.transpose(norm_t[:, e, t, :], tiles["norm", b][:, t, 2 * u + e, :], ident_f32[:])
            tiles["norm_t", b, u] = norm_t

        def gain_and_biases(b, q):
            if q == 0:
                gn = work.tile([P, PACK, TILES, P], F32)
                tiles["gn", b] = gn
            nc.scalar.activation(
                out=tiles["gn", b][:, q, :, :],
                in_=tiles["norm_t", b, q // 2][:, q % 2, :, :],
                func=ACT.Identity,
                scale=gain[:, q : q + 1],
                bias=shift[:, q : q + 1],
            )

        def skip_product(b, t):
            rows = slice(t * P, (t + 1) * P)
            skip_t = psum_skip.tile([P, PACK, P], F32)
            for q in range(PACK):
                cols = slice(q * P, (q + 1) * P)
                nc.tensor.matmul_mx(
                    out=skip_t[:, q, :],
                    lhsT=skip_codes[:, cols].bitcast(FP8X4),
                    lhsT_scale=skip_scales[:, cols],
                    rhs=tiles["xc_codes", b][:, rows].bitcast(FP8X4),
                    rhs_scale=tiles["xc_scales", b][:, rows],
                    start=True,
                    stop=True,
                )
            tiles["skip_t", b, t] = skip_t

        def add_streams(b, t):
            if t == 0:
                summed = work.tile([P, TILES, P, PACK], F32)
                tiles["summed", b] = summed
            nc.vector.tensor_tensor(
                out=tiles["summed", b][:, t, :, :].rearrange("p (c i) q -> p c q i", i=LINE),
                in0=tiles["skip_t", b, t][:].rearrange("p q (c i) -> p c q i", i=LINE),
                in1=tiles["gn", b][:, :, t, :].rearrange("p q (c i) -> p c q i", i=LINE),
                op=ALU.add,
            )

        def apply_gate(b):
            g_grouped = work.tile([P, TILES, P, PACK], BF16, align_bytes=64)
            nc.vector.tensor_tensor(out=g_grouped[:], in0=tiles["summed", b][:], in1=tiles["gate", b][:], op=ALU.mult)
            tiles["g_grouped", b] = g_grouped

        def quantise_g(b):
            g_codes = work.tile([P, TILES * P], U32, align_bytes=64)
            g_scales = work.tile([P, TILES * P], U8, align_bytes=64)
            quantise(nc, g_codes[:], g_scales[:], tiles["g_grouped", b][:].rearrange("p t r q -> p (t r q)"))
            tiles["g_codes", b], tiles["g_scales", b] = g_codes, g_scales

        def down_product(b):
            y = psum_y.tile([P, TILES, IN], F32)
            for t in range(TILES):
                rows = slice(t * P, (t + 1) * P)
                nc.tensor.matmul_mx(
                    out=y[:, t, :],
                    lhsT=tiles["g_codes", b][:, rows].bitcast(FP8X4),
                    lhsT_scale=tiles["g_scales", b][:, rows],
                    rhs=down_codes[:].bitcast(FP8X4),
                    rhs_scale=down_scales[:],
                    start=True,
                    stop=True,
                )
            tiles["y", b] = y

        def add_residual_and_store(b):
            result = work.tile([P, TILES, IN], F32)
            nc.vector.tensor_tensor(out=result[:], in0=tiles["y", b][:], in1=tiles["residual", b][:], op=ALU.add)
            nc.sync.dma_start(out=out_blocks[b], in_=result[:])

        def run(piece, b, *part):
            if 0 <= b < N_BLOCKS:
                piece(b, *part)

        def turn(i):
            run(load, i + 3)
            run(skip_product, i - 1, 0)
            run(skip_product, i - 1, 1)
            run(transpose_words, i + 2, "xc")
            run(transpose_words, i + 2, "xr")
            run(transpose_norm, i, 0)
            run(transpose_norm, i, 1)
            run(down_product, i - 2)
            run(group_x_conv, i + 2)
            for t in range(TILES):
                run(silu_gate, i + 2, t)
            for q in range(PACK):
                run(gain_and_biases, i, q)
            for t in range(TILES):
                run(normalise, i + 1, t)
            run(group_stats, i + 2)
            run(rstd_and_residual, i + 2)
            run(add_streams, i - 1, 0)
            run(add_streams, i - 1, 1)
            run(add_residual_and_store, i - 2)
            run(apply_gate, i - 1)
            run(quantise_x_conv, i + 2)
            run(quantise_g, i - 1)

        with tc.manual_schedule():
            turn(-3)
            turn(-2)
            prepare_weights()
            for i in range(-1, N_BLOCKS + 2):
                turn(i)
